import numpy as np
import ml_dtypes


def mxq(x, axis, fmt="e4m3"):
    dtype, down = {"e4m3": (ml_dtypes.float8_e4m3fn, 7), "e5m2": (ml_dtypes.float8_e5m2, 14)}[fmt]
    v = np.moveaxis(np.asarray(x, np.float32).astype(ml_dtypes.bfloat16).astype(np.float64), axis, -1)
    blocks = v.reshape(v.shape[:-1] + (-1, 32))
    amax = np.abs(blocks).max(-1, keepdims=True)
    byte = np.maximum(np.where(amax > 0, np.frexp(amax)[1] - 1 + 127, 0) - down, 1)
    scale = np.exp2(byte - 127.0)
    codes = (blocks / scale).astype(np.float32).astype(dtype).astype(np.float64)
    return np.moveaxis((codes * scale).reshape(v.shape), -1, axis)


WIDE = False


def mx_kscale(k):
    if not WIDE:
        return np.ones(k)
    levels = np.array([10, -10, 5, -5, 0])
    a = np.random.permutation(np.resize(levels, k // 512 * 4)).reshape(k // 512, 4)
    idx = np.arange(k)
    return np.exp2(a[idx // 512, idx % 128 // 32])


BF16 = ml_dtypes.bfloat16


def bf(x):
    return np.asarray(x, np.float32).astype(BF16)


def f64(x):
    return np.asarray(x).astype(np.float64)


B, S, D, H, DH, F = 2, 128, 2048, 16, 128, 4096
E = H * DH
EPS = 1e-5


def layernorm(x, g, b):
    mu = x.mean(-1, keepdims=True)
    var = np.square(x - mu).mean(-1, keepdims=True)
    return (x - mu) / np.sqrt(var + EPS) * g + b


def make_pe():
    position = np.arange(S)[:, None] * 1.0
    div_term = np.exp(np.arange(0, DH, 2) * -(np.log(10000.0) / DH))
    pe = np.zeros((S, DH))
    pe[:, 0::2] = np.sin(position * div_term)
    pe[:, 1::2] = np.cos(position * div_term)
    return pe


def rope(t, pe):
    tr = t.reshape(B, H, S, DH // 2, 2)
    c = pe[:S, 0::2][None, None]
    d = pe[:S, 1::2][None, None]
    t0 = tr[..., 0] * c - tr[..., 1] * d
    t1 = tr[..., 0] * d + tr[..., 1] * c
    return np.stack([t0, t1], axis=-1).reshape(B, H, S, DH)


def setup_inputs():
    s = mx_kscale(D)
    x = np.random.standard_normal((B, S, D)) + 0.5 * np.random.standard_normal((B, S, 1))
    return {"x": bf(x),
            "pe": bf(make_pe()),
            "w_qkv": bf(np.random.standard_normal((3 * E, D)) / np.sqrt(D) / s),
            "g1": bf((1.0 + 0.1 * np.random.standard_normal(D)) * s),
            "b1": bf(0.1 * np.random.standard_normal(D) * s)}


def reference(x, pe, w_qkv, g1, b1):
    h = layernorm(f64(x), f64(g1), f64(b1))
    qkv = mxq(h, 2, "e4m3") @ mxq(f64(w_qkv), 1, "e4m3").T
    qkv = qkv.reshape(B, S, 3, H, DH)
    q, k, v = [qkv[:, :, i].transpose(0, 2, 1, 3) for i in range(3)]
    p = f64(pe)
    return rope(q, p), rope(k, p), v

@@ -1,0 +1,267 @@
+from contextlib import ExitStack
+
+import concourse.mybir as mybir
+from concourse.masks import make_identity
+
+F32 = mybir.dt.float32
+BF16 = mybir.dt.bfloat16
+I32 = mybir.dt.int32
+U32 = mybir.dt.uint32
+U8 = mybir.dt.uint8
+FP8X4 = mybir.dt.float8_e4m3fn_x4
+ALU = mybir.AluOpType
+
+P = 128
+BATCH = 2
+D = 2048
+HEADS = 16
+E = HEADS * P
+EPS = 1e-5
+PACK = 4
+PASSES = D // (P * PACK)
+BANK = 512
+GROUP = BANK
+ROWS = GROUP // P
+GROUP_HEADS = GROUP // P
+WORDS = D // 2
+PREFETCH = 4
+AHEAD = 2
+
+FLOPS = 2 * BATCH * P * D * 3 * E
+
+
+def tile_minitransformerlayer_pa_kernel(tc, x, pe, w_qkv, g1, b1, out_0, out_1, out_2):
+    nc = tc.nc
+    outs = (out_0, out_1, out_2)
+    groups = [(part, head_group) for head_group in range(HEADS // GROUP_HEADS) for part in range(3)]
+
+    with ExitStack() as ctx:
+        const = ctx.enter_context(tc.tile_pool(name="const", bufs=1))
+        norm = ctx.enter_context(tc.tile_pool(name="norm", bufs=BATCH))
+        raw_pool = ctx.enter_context(tc.tile_pool(name="raw", bufs=PREFETCH))
+        grouped_pool = ctx.enter_context(tc.tile_pool(name="grouped", bufs=2 * PASSES))
+        codes_pool = ctx.enter_context(tc.tile_pool(name="codes", bufs=3))
+        rot_pool = ctx.enter_context(tc.tile_pool(name="rot", bufs=2))
+        result_pool = ctx.enter_context(tc.tile_pool(name="result", bufs=8))
+        psum = ctx.enter_context(tc.psum_pool(name="psum", bufs=4))
+        ctx.enter_context(tc.manual_schedule())
+
+        one = const.tile([P, 1], F32)
+        nc.vector.memset(one[:], 1.0)
+        warm = const.tile([P, 1], F32)
+        nc.scalar.sqrt(out=warm[:], in_=one[:])
+        ones = const.tile([P, P], BF16)
+        nc.vector.memset(ones[:], 1.0)
+        gain_row = const.tile([P, D], BF16)
+        bias_row = const.tile([P, D], BF16)
+        nc.vector.memset(gain_row[:].bitcast(I32), 0)
+        nc.vector.memset(bias_row[:].bitcast(I32), 0)
+        pe_sb = const.tile([P, P], BF16)
+        ident_f32 = const.tile([P, P], F32)
+        make_identity(nc, ident_f32[:])
+        ident_bf16 = const.tile([P, P], BF16)
+        make_identity(nc, ident_bf16[:])
+
+        x_sb = {}
+        for b in range(BATCH):
+            x_tile = norm.tile([P, D], BF16, name="x_tile")
+            nc.sync.dma_start(out=x_tile[:], in_=x[b])
+            x_sb[b] = x_tile
+        nc.sync.dma_start(out=gain_row[0:1, :], in_=g1.rearrange("(o d) -> o d", o=1))
+        nc.sync.dma_start(out=bias_row[0:1, :], in_=b1.rearrange("(o d) -> o d", o=1))
+        nc.sync.dma_start(out=pe_sb[:], in_=pe)
+
+        w_raw = {}
+
+        def load_weights(n):
+            part, head_group = groups[n]
+            first = part * E + head_group * GROUP
+            raw = raw_pool.tile([P, ROWS * D], BF16, name="raw")
+            nc.sync.dma_start(
+                out=raw[:], in_=w_qkv[first : first + GROUP, :].rearrange("(p r) k -> p (r k)", r=ROWS)
+            )
+            w_raw[n] = raw
+
+        for n in range(PREFETCH):
+            load_weights(n)
+
+        pe_heads = pe_sb[:].unsqueeze(1).to_broadcast([P, GROUP_HEADS, P])
+        pe_pairs = (
+            pe_sb[:].rearrange("p (j i) -> p j i", i=2).unsqueeze(1).to_broadcast([P, GROUP_HEADS, P // 2, 2])
+        )
+        table_a = const.tile([P, GROUP_HEADS, P], F32)
+        nc.gpsimd.tensor_copy(out=table_a[:], in_=pe_heads)
+        table_b = const.tile([P, GROUP_HEADS, P // 2, 2], F32)
+        nc.gpsimd.tensor_scalar(
+            out=table_b[:, :, :, 0], in0=pe_pairs[:, :, :, 1], scalar1=-1.0, scalar2=0.0, op0=ALU.mult, op1=ALU.add
+        )
+        nc.gpsimd.tensor_copy(out=table_b[:, :, :, 1], in_=pe_pairs[:, :, :, 0])
+
+        def repeat_on_partitions(row, name):
+            repeated = const.tile([P, D], BF16, name=name)
+            for c in range(D // BANK):
+                cols = slice(c * BANK, (c + 1) * BANK)
+                spread = psum.tile([P, BANK], F32, tag="acc", name="spread")
+                nc.tensor.matmul(out=spread[:], lhsT=ones[:], rhs=row[:, cols], start=True, stop=True)
+                nc.scalar.copy(out=repeated[:, cols], in_=spread[:])
+            return repeated
+
+        gain = repeat_on_partitions(gain_row, "gain")
+        bias = repeat_on_partitions(bias_row, "bias")
+
+        mean_var = {}
+        std = {}
+
+        def token_statistics(b):
+            stats = norm.tile([P, D // BANK, 6], F32, name="stats")
+            for c in range(D // BANK):
+                nc.vector.bn_stats(out=stats[:, c, :], in_=x_sb[b][:, c * BANK : (c + 1) * BANK])
+            mv = norm.tile([P, 2], F32, name="mv")
+            nc.vector.bn_aggr(out=mv[:], in_=stats[:].rearrange("p c s -> p (c s)"))
+            var_eps = norm.tile([P, 1], F32, name="var_eps")
+            nc.vector.tensor_scalar_add(out=var_eps[:], in0=mv[:, 1:2], scalar1=EPS)
+            root = norm.tile([P, 1], F32, name="root")
+            nc.scalar.sqrt(out=root[:], in_=var_eps[:])
+            mean_var[b] = mv
+            std[b] = root
+
+        h_sorted = {}
+
+        def normalise(b):
+            centred = norm.tile([P, D], F32, name="centred")
+            nc.vector.scalar_tensor_tensor(
+                out=centred[:], in0=x_sb[b][:], scalar=mean_var[b][:, 0:1], in1=gain[:], op0=ALU.subtract, op1=ALU.mult
+            )
+            rstd = norm.tile([P, 1], F32, name="rstd")
+            nc.vector.reciprocal(out=rstd[:], in_=std[b][:])
+            h_tile = norm.tile([P, 2 * PASSES, 2, P], BF16, name="h_tile")
+            for e in range(2):
+                nc.vector.scalar_tensor_tensor(
+                    out=h_tile[:, :, e, :],
+                    in0=centred[:].rearrange("p (cu q e) -> p cu e q", q=P, e=2)[:, :, e, :],
+                    scalar=rstd[:],
+                    in1=bias[:].rearrange("p (cu q e) -> p cu e q", q=P, e=2)[:, :, e, :],
+                    op0=ALU.mult,
+                    op1=ALU.add,
+                )
+            h_sorted[b] = h_tile
+
+        h_grouped = const.tile([P, BATCH, PASSES, P, PACK], BF16, align_bytes=64)
+        h_codes = const.tile([P, BATCH, PASSES * P], U32, align_bytes=64)
+        h_scales = const.tile([P, BATCH, PASSES * P], U8, align_bytes=64)
+
+        def transpose_and_quantise_h(b):
+            for c in range(PASSES):
+                flipped_h = psum.tile([P, PACK, P], BF16, tag="acc", name="flipped_h")
+                for u in range(2):
+                    for e in range(2):
+                        nc.tensor.transpose(flipped_h[:, 2 * u + e, :], h_sorted[b][:, 2 * c + u, e, :], ident_bf16[:])
+                nc.scalar.copy(out=h_grouped[:, b, c, :, :], in_=flipped_h[:].rearrange("p t r -> p r t"))
+            nc.vector.quantize_mx(
+                out=h_codes[:, b, :].bitcast(FP8X4),
+                scales=h_scales[:, b, :],
+                in_=h_grouped[:, b].rearrange("p c r t -> p (c r t)"),
+            )
+
+        w_grouped = {}
+
+        def transpose_weights(n):
+            words = w_raw[n][:].bitcast(F32)
+            for c in range(PASSES):
+                grouped = grouped_pool.tile([P, GROUP * PACK], BF16, align_bytes=64, name="grouped")
+                grouped_words = grouped[:].bitcast(F32)
+                for half in range(2):
+                    flipped = psum.tile([P, 2, BANK // 2], F32, tag="flipped", name="flipped")
+                    for u in range(2):
+                        for r in range(2):
+                            first = (2 * half + r) * WORDS + (2 * c + u) * P
+                            nc.tensor.transpose(
+                                flipped[:, u, r * P : (r + 1) * P], words[:, first : first + P], ident_f32[:]
+                            )
+                    nc.scalar.copy(
+                        out=grouped_words[:, half * BANK : (half + 1) * BANK].rearrange("p (n u) -> p n u", u=2),
+                        in_=flipped[:].rearrange("p u n -> p n u"),
+                    )
+                w_grouped[(n, c)] = grouped
+            if n + PREFETCH < len(groups):
+                load_weights(n + PREFETCH)
+
+        w_codes = {}
+        w_scales = {}
+
+        def quantise_weights(n):
+            codes = codes_pool.tile([P, PASSES, GROUP], U32, align_bytes=64, name="codes")
+            scales = codes_pool.tile([P, PASSES, GROUP], U8, align_bytes=64, name="scales")
+            for c in range(PASSES):
+                nc.vector.quantize_mx(
+                    out=codes[:, c, :].bitcast(FP8X4), scales=scales[:, c, :], in_=w_grouped[(n, c)][:]
+                )
+            w_codes[n] = codes
+            w_scales[n] = scales
+
+        products = {}
+
+        def multiply(n):
+            for b in range(BATCH):
+                acc = psum.tile([P, BANK], F32, tag="acc", name="acc")
+                for c in range(PASSES):
+                    tokens = slice(c * P, (c + 1) * P)
+                    nc.tensor.matmul_mx(
+                        out=acc[:],
+                        lhsT=h_codes[:, b, tokens].bitcast(FP8X4),
+                        lhsT_scale=h_scales[:, b, tokens],
+                        rhs=w_codes[n][:, c, :].bitcast(FP8X4),
+                        rhs_scale=w_scales[n][:, c, :],
+                        start=(c == 0),
+                        stop=(c == PASSES - 1),
+                    )
+                products[(n, b)] = acc
+
+        def finish(n):
+            part, head_group = groups[n]
+            heads = slice(head_group * GROUP_HEADS, (head_group + 1) * GROUP_HEADS)
+            for b in range(BATCH):
+                acc = products[(n, b)]
+                result = result_pool.tile([P, GROUP], F32, name="result")
+                if part == 2:
+                    nc.scalar.copy(
+                        out=result[:].rearrange("s (p r) -> s p r", r=ROWS),
+                        in_=acc[:].rearrange("s (r p) -> s p r", r=ROWS),
+                    )
+                else:
+                    pairs = acc[:].rearrange("s (v i p) -> s i p v", v=2, i=2)
+                    shape = [P, P, 2, 2]
+                    from_a = rot_pool.tile([P, GROUP], F32, name="from_a")
+                    nc.vector.tensor_mul(
+                        out=from_a[:].rearrange("s (p v i) -> s p v i", v=2, i=2),
+                        in0=pairs[:, 0].unsqueeze(3).to_broadcast(shape),
+                        in1=table_a[:].rearrange("s h (q v i) -> s (h q) v i", v=2, i=2),
+                    )
+                    from_b = rot_pool.tile([P, GROUP], F32, name="from_b")
+                    nc.vector.tensor_mul(
+                        out=from_b[:].rearrange("s (p v i) -> s p v i", v=2, i=2),
+                        in0=pairs[:, 1].unsqueeze(3).to_broadcast(shape),
+                        in1=table_b[:].rearrange("s h (q v) i -> s (h q) v i", v=2),
+                    )
+                    nc.vector.tensor_add(out=result[:], in0=from_a[:], in1=from_b[:])
+                nc.gpsimd.dma_start(
+                    out=outs[part][b, heads].rearrange("h s d -> s h d"),
+                    in_=result[:].rearrange("s (h d) -> s h d", d=P),
+                )
+
+        token_statistics(0)
+        token_statistics(1)
+        transpose_weights(0)
+        normalise(0)
+        normalise(1)
+        transpose_and_quantise_h(0)
+        transpose_and_quantise_h(1)
+        transpose_weights(1)
+        quantise_weights(0)
+        quantise_weights(1)
+        for n in range(len(groups)):
+            multiply(n)
+            finish(n)
+            if n + AHEAD < len(groups):
+                transpose_weights(n + AHEAD)
+                quantise_weights(n + AHEAD)

@@ -26,6 +26,7 @@ GROUP_HEADS = GROUP // P
 WORDS = D // 2
 PREFETCH = 4
 AHEAD = 2
+HALF = PASSES // 2
 
 FLOPS = 2 * BATCH * P * D * 3 * E
 
@@ -39,11 +40,12 @@ def tile_minitransformerlayer_pa_kernel(tc, x, pe, w_qkv, g1, b1, out_0, out_1, 
         const = ctx.enter_context(tc.tile_pool(name="const", bufs=1))
         norm = ctx.enter_context(tc.tile_pool(name="norm", bufs=BATCH))
         raw_pool = ctx.enter_context(tc.tile_pool(name="raw", bufs=PREFETCH))
-        grouped_pool = ctx.enter_context(tc.tile_pool(name="grouped", bufs=2 * PASSES))
-        codes_pool = ctx.enter_context(tc.tile_pool(name="codes", bufs=3))
+        grouped_pool = ctx.enter_context(tc.tile_pool(name="grouped", bufs=4))
+        codes_pool = ctx.enter_context(tc.tile_pool(name="codes", bufs=6))
         rot_pool = ctx.enter_context(tc.tile_pool(name="rot", bufs=2))
         result_pool = ctx.enter_context(tc.tile_pool(name="result", bufs=8))
-        psum = ctx.enter_context(tc.psum_pool(name="psum", bufs=4))
+        flip_psum = ctx.enter_context(tc.psum_pool(name="flip_psum", bufs=6))
+        acc_psum = ctx.enter_context(tc.psum_pool(name="acc_psum", bufs=2))
         ctx.enter_context(tc.manual_schedule())
 
         one = const.tile([P, 1], F32)
@@ -101,7 +103,7 @@ def tile_minitransformerlayer_pa_kernel(tc, x, pe, w_qkv, g1, b1, out_0, out_1, 
             repeated = const.tile([P, D], BF16, name=name)
             for c in range(D // BANK):
                 cols = slice(c * BANK, (c + 1) * BANK)
-                spread = psum.tile([P, BANK], F32, tag="acc", name="spread")
+                spread = flip_psum.tile([P, BANK], F32, tag="flipped", name="spread")
                 nc.tensor.matmul(out=spread[:], lhsT=ones[:], rhs=row[:, cols], start=True, stop=True)
                 nc.scalar.copy(out=repeated[:, cols], in_=spread[:])
             return repeated
@@ -152,7 +154,7 @@ def tile_minitransformerlayer_pa_kernel(tc, x, pe, w_qkv, g1, b1, out_0, out_1, 
 
         def transpose_and_quantise_h(b):
             for c in range(PASSES):
-                flipped_h = psum.tile([P, PACK, P], BF16, tag="acc", name="flipped_h")
+                flipped_h = flip_psum.tile([P, PACK, P], BF16, tag="flipped", name="flipped_h")
                 for u in range(2):
                     for e in range(2):
                         nc.tensor.transpose(flipped_h[:, 2 * u + e, :], h_sorted[b][:, 2 * c + u, e, :], ident_bf16[:])
@@ -165,103 +167,106 @@ def tile_minitransformerlayer_pa_kernel(tc, x, pe, w_qkv, g1, b1, out_0, out_1, 
 
         w_grouped = {}
 
-        def transpose_weights(n):
+        def transpose_weights(n, half):
             words = w_raw[n][:].bitcast(F32)
-            for c in range(PASSES):
-                grouped = grouped_pool.tile([P, GROUP * PACK], BF16, align_bytes=64, name="grouped")
-                grouped_words = grouped[:].bitcast(F32)
-                for half in range(2):
-                    flipped = psum.tile([P, 2, BANK // 2], F32, tag="flipped", name="flipped")
+            grouped = grouped_pool.tile([P, HALF, GROUP * PACK], BF16, align_bytes=64, name="grouped")
+            for c in range(HALF):
+                grouped_words = grouped[:, c, :].bitcast(F32)
+                for side in range(2):
+                    flipped = flip_psum.tile([P, 2, BANK // 2], F32, tag="flipped", name="flipped")
                     for u in range(2):
                         for r in range(2):
-                            first = (2 * half + r) * WORDS + (2 * c + u) * P
+                            first = (2 * side + r) * WORDS + (2 * (half * HALF + c) + u) * P
                             nc.tensor.transpose(
                                 flipped[:, u, r * P : (r + 1) * P], words[:, first : first + P], ident_f32[:]
                             )
                     nc.scalar.copy(
-                        out=grouped_words[:, half * BANK : (half + 1) * BANK].rearrange("p (n u) -> p n u", u=2),
+                        out=grouped_words[:, side * BANK : (side + 1) * BANK].rearrange("p (n u) -> p n u", u=2),
                         in_=flipped[:].rearrange("p u n -> p n u"),
                     )
-                w_grouped[(n, c)] = grouped
-            if n + PREFETCH < len(groups):
+            w_grouped[(n, half)] = grouped
+            if half == 1 and n + PREFETCH < len(groups):
                 load_weights(n + PREFETCH)
 
         w_codes = {}
         w_scales = {}
 
-        def quantise_weights(n):
-            codes = codes_pool.tile([P, PASSES, GROUP], U32, align_bytes=64, name="codes")
-            scales = codes_pool.tile([P, PASSES, GROUP], U8, align_bytes=64, name="scales")
-            for c in range(PASSES):
-                nc.vector.quantize_mx(
-                    out=codes[:, c, :].bitcast(FP8X4), scales=scales[:, c, :], in_=w_grouped[(n, c)][:]
-                )
-            w_codes[n] = codes
-            w_scales[n] = scales
+        def quantise_weights(n, half):
+            codes = codes_pool.tile([P, HALF, GROUP], U32, align_bytes=64, name="codes")
+            scales = codes_pool.tile([P, HALF, GROUP], U8, align_bytes=64, name="scales")
+            nc.vector.quantize_mx(
+                out=codes[:].rearrange("p c n -> p (c n)").bitcast(FP8X4),
+                scales=scales[:].rearrange("p c n -> p (c n)"),
+                in_=w_grouped[(n, half)][:].rearrange("p c n -> p (c n)"),
+            )
+            w_codes[(n, half)] = codes
+            w_scales[(n, half)] = scales
 
         products = {}
 
-        def multiply(n):
-            for b in range(BATCH):
-                acc = psum.tile([P, BANK], F32, tag="acc", name="acc")
-                for c in range(PASSES):
-                    tokens = slice(c * P, (c + 1) * P)
-                    nc.tensor.matmul_mx(
-                        out=acc[:],
-                        lhsT=h_codes[:, b, tokens].bitcast(FP8X4),
-                        lhsT_scale=h_scales[:, b, tokens],
-                        rhs=w_codes[n][:, c, :].bitcast(FP8X4),
-                        rhs_scale=w_scales[n][:, c, :],
-                        start=(c == 0),
-                        stop=(c == PASSES - 1),
-                    )
-                products[(n, b)] = acc
+        def multiply(n, b):
+            acc = acc_psum.tile([P, BANK], F32, name="acc")
+            for c in range(PASSES):
+                tokens = slice(c * P, (c + 1) * P)
+                nc.tensor.matmul_mx(
+                    out=acc[:],
+                    lhsT=h_codes[:, b, tokens].bitcast(FP8X4),
+                    lhsT_scale=h_scales[:, b, tokens],
+                    rhs=w_codes[(n, c // HALF)][:, c % HALF, :].bitcast(FP8X4),
+                    rhs_scale=w_scales[(n, c // HALF)][:, c % HALF, :],
+                    start=(c == 0),
+                    stop=(c == PASSES - 1),
+                )
+            products[(n, b)] = acc
 
-        def finish(n):
+        def finish(n, b):
             part, head_group = groups[n]
             heads = slice(head_group * GROUP_HEADS, (head_group + 1) * GROUP_HEADS)
-            for b in range(BATCH):
-                acc = products[(n, b)]
-                result = result_pool.tile([P, GROUP], F32, name="result")
-                if part == 2:
-                    nc.scalar.copy(
-                        out=result[:].rearrange("s (p r) -> s p r", r=ROWS),
-                        in_=acc[:].rearrange("s (r p) -> s p r", r=ROWS),
-                    )
-                else:
-                    pairs = acc[:].rearrange("s (v i p) -> s i p v", v=2, i=2)
-                    shape = [P, P, 2, 2]
-                    from_a = rot_pool.tile([P, GROUP], F32, name="from_a")
-                    nc.vector.tensor_mul(
-                        out=from_a[:].rearrange("s (p v i) -> s p v i", v=2, i=2),
-                        in0=pairs[:, 0].unsqueeze(3).to_broadcast(shape),
-                        in1=table_a[:].rearrange("s h (q v i) -> s (h q) v i", v=2, i=2),
-                    )
-                    from_b = rot_pool.tile([P, GROUP], F32, name="from_b")
-                    nc.vector.tensor_mul(
-                        out=from_b[:].rearrange("s (p v i) -> s p v i", v=2, i=2),
-                        in0=pairs[:, 1].unsqueeze(3).to_broadcast(shape),
-                        in1=table_b[:].rearrange("s h (q v) i -> s (h q) v i", v=2),
-                    )
-                    nc.vector.tensor_add(out=result[:], in0=from_a[:], in1=from_b[:])
-                nc.gpsimd.dma_start(
-                    out=outs[part][b, heads].rearrange("h s d -> s h d"),
-                    in_=result[:].rearrange("s (h d) -> s h d", d=P),
+            acc = products[(n, b)]
+            result = result_pool.tile([P, GROUP], F32, name="result")
+            if part == 2:
+                nc.scalar.copy(
+                    out=result[:].rearrange("s (p r) -> s p r", r=ROWS),
+                    in_=acc[:].rearrange("s (r p) -> s p r", r=ROWS),
                 )
+            else:
+                pairs = acc[:].rearrange("s (v i p) -> s i p v", v=2, i=2)
+                shape = [P, P, 2, 2]
+                from_a = rot_pool.tile([P, GROUP], F32, name="from_a")
+                nc.vector.tensor_mul(
+                    out=from_a[:].rearrange("s (p v i) -> s p v i", v=2, i=2),
+                    in0=pairs[:, 0].unsqueeze(3).to_broadcast(shape),
+                    in1=table_a[:].rearrange("s h (q v i) -> s (h q) v i", v=2, i=2),
+                )
+                from_b = rot_pool.tile([P, GROUP], F32, name="from_b")
+                nc.vector.tensor_mul(
+                    out=from_b[:].rearrange("s (p v i) -> s p v i", v=2, i=2),
+                    in0=pairs[:, 1].unsqueeze(3).to_broadcast(shape),
+                    in1=table_b[:].rearrange("s h (q v) i -> s (h q) v i", v=2),
+                )
+                nc.vector.tensor_add(out=result[:], in0=from_a[:], in1=from_b[:])
+            nc.gpsimd.dma_start(
+                out=outs[part][b, heads].rearrange("h s d -> s h d"),
+                in_=result[:].rearrange("s (h d) -> s h d", d=P),
+            )
 
         token_statistics(0)
         token_statistics(1)
-        transpose_weights(0)
+        transpose_weights(0, 0)
+        transpose_weights(0, 1)
         normalise(0)
         normalise(1)
         transpose_and_quantise_h(0)
         transpose_and_quantise_h(1)
-        transpose_weights(1)
-        quantise_weights(0)
-        quantise_weights(1)
+        transpose_weights(1, 0)
+        transpose_weights(1, 1)
+        for n in range(AHEAD):
+            for half in range(2):
+                quantise_weights(n, half)
         for n in range(len(groups)):
-            multiply(n)
-            finish(n)
-            if n + AHEAD < len(groups):
-                transpose_weights(n + AHEAD)
-                quantise_weights(n + AHEAD)
+            for step in range(BATCH):
+                multiply(n, step)
+                finish(n, step)
+                if n + AHEAD < len(groups):
+                    transpose_weights(n + AHEAD, step)
+                    quantise_weights(n + AHEAD, step)

@@ -27,6 +27,7 @@ WORDS = D // 2
 PREFETCH = 4
 AHEAD = 2
 HALF = PASSES // 2
+LAG = 2
 
 FLOPS = 2 * BATCH * P * D * 3 * E
 
@@ -42,7 +43,7 @@ def tile_minitransformerlayer_pa_kernel(tc, x, pe, w_qkv, g1, b1, out_0, out_1, 
         raw_pool = ctx.enter_context(tc.tile_pool(name="raw", bufs=PREFETCH))
         grouped_pool = ctx.enter_context(tc.tile_pool(name="grouped", bufs=4))
         codes_pool = ctx.enter_context(tc.tile_pool(name="codes", bufs=6))
-        rot_pool = ctx.enter_context(tc.tile_pool(name="rot", bufs=2))
+        rot_pool = ctx.enter_context(tc.tile_pool(name="rot", bufs=3))
         result_pool = ctx.enter_context(tc.tile_pool(name="result", bufs=8))
         flip_psum = ctx.enter_context(tc.psum_pool(name="flip_psum", bufs=6))
         acc_psum = ctx.enter_context(tc.psum_pool(name="acc_psum", bufs=2))
@@ -152,13 +153,15 @@ def tile_minitransformerlayer_pa_kernel(tc, x, pe, w_qkv, g1, b1, out_0, out_1, 
         h_codes = const.tile([P, BATCH, PASSES * P], U32, align_bytes=64)
         h_scales = const.tile([P, BATCH, PASSES * P], U8, align_bytes=64)
 
-        def transpose_and_quantise_h(b):
+        def transpose_h(b):
             for c in range(PASSES):
                 flipped_h = flip_psum.tile([P, PACK, P], BF16, tag="flipped", name="flipped_h")
                 for u in range(2):
                     for e in range(2):
                         nc.tensor.transpose(flipped_h[:, 2 * u + e, :], h_sorted[b][:, 2 * c + u, e, :], ident_bf16[:])
                 nc.scalar.copy(out=h_grouped[:, b, c, :, :], in_=flipped_h[:].rearrange("p t r -> p r t"))
+
+        def quantise_h(b):
             nc.vector.quantize_mx(
                 out=h_codes[:, b, :].bitcast(FP8X4),
                 scales=h_scales[:, b, :],
@@ -225,7 +228,7 @@ def tile_minitransformerlayer_pa_kernel(tc, x, pe, w_qkv, g1, b1, out_0, out_1, 
             acc = products[(n, b)]
             result = result_pool.tile([P, GROUP], F32, name="result")
             if part == 2:
-                nc.scalar.copy(
+                nc.vector.tensor_copy(
                     out=result[:].rearrange("s (p r) -> s p r", r=ROWS),
                     in_=acc[:].rearrange("s (r p) -> s p r", r=ROWS),
                 )
@@ -244,29 +247,32 @@ def tile_minitransformerlayer_pa_kernel(tc, x, pe, w_qkv, g1, b1, out_0, out_1, 
                     in0=pairs[:, 1].unsqueeze(3).to_broadcast(shape),
                     in1=table_b[:].rearrange("s h (q v) i -> s (h q) v i", v=2),
                 )
-                nc.vector.tensor_add(out=result[:], in0=from_a[:], in1=from_b[:])
-            nc.gpsimd.dma_start(
+                nc.gpsimd.tensor_add(out=result[:], in0=from_a[:], in1=from_b[:])
+            nc.sync.dma_start(
                 out=outs[part][b, heads].rearrange("h s d -> s h d"),
                 in_=result[:].rearrange("s (h d) -> s h d", d=P),
             )
 
+        halves = [(n, half) for n in range(len(groups)) for half in range(2)]
         token_statistics(0)
         token_statistics(1)
         transpose_weights(0, 0)
         transpose_weights(0, 1)
         normalise(0)
-        normalise(1)
-        transpose_and_quantise_h(0)
-        transpose_and_quantise_h(1)
+        transpose_h(0)
         transpose_weights(1, 0)
         transpose_weights(1, 1)
-        for n in range(AHEAD):
-            for half in range(2):
-                quantise_weights(n, half)
-        for n in range(len(groups)):
-            for step in range(BATCH):
-                multiply(n, step)
-                finish(n, step)
-                if n + AHEAD < len(groups):
-                    transpose_weights(n + AHEAD, step)
-                    quantise_weights(n + AHEAD, step)
+        normalise(1)
+        transpose_h(1)
+        quantise_weights(0, 0)
+        quantise_weights(0, 1)
+        quantise_h(0)
+        quantise_h(1)
+        for t in range(len(halves)):
+            n, b = halves[t]
+            multiply(n, b)
+            if t + 2 * AHEAD - LAG < len(halves):
+                quantise_weights(*halves[t + 2 * AHEAD - LAG])
+            finish(n, b)
+            if t + 2 * AHEAD < len(halves):
+                transpose_weights(*halves[t + 2 * AHEAD])

@@ -20,13 +20,12 @@ EPS = 1e-5
 PACK = 4
 PASSES = D // (P * PACK)
 BANK = 512
-GROUP = BANK
+WORDS = D // 2
+GROUP = BANK // BATCH
 ROWS = GROUP // P
 GROUP_HEADS = GROUP // P
-WORDS = D // 2
-PREFETCH = 4
-AHEAD = 2
-HALF = PASSES // 2
+PREFETCH = 10
+AHEAD = 4
 LAG = 2
 
 FLOPS = 2 * BATCH * P * D * 3 * E
@@ -35,14 +34,14 @@ FLOPS = 2 * BATCH * P * D * 3 * E
 def tile_minitransformerlayer_pa_kernel(tc, x, pe, w_qkv, g1, b1, out_0, out_1, out_2):
     nc = tc.nc
     outs = (out_0, out_1, out_2)
-    groups = [(part, head_group) for head_group in range(HEADS // GROUP_HEADS) for part in range(3)]
+    groups = [(part, pair) for pair in range(HEADS // GROUP_HEADS) for part in range(3)]
 
     with ExitStack() as ctx:
         const = ctx.enter_context(tc.tile_pool(name="const", bufs=1))
         norm = ctx.enter_context(tc.tile_pool(name="norm", bufs=BATCH))
         raw_pool = ctx.enter_context(tc.tile_pool(name="raw", bufs=PREFETCH))
-        grouped_pool = ctx.enter_context(tc.tile_pool(name="grouped", bufs=4))
-        codes_pool = ctx.enter_context(tc.tile_pool(name="codes", bufs=6))
+        grouped_pool = ctx.enter_context(tc.tile_pool(name="grouped", bufs=AHEAD))
+        codes_pool = ctx.enter_context(tc.tile_pool(name="codes", bufs=AHEAD))
         rot_pool = ctx.enter_context(tc.tile_pool(name="rot", bufs=3))
         result_pool = ctx.enter_context(tc.tile_pool(name="result", bufs=8))
         flip_psum = ctx.enter_context(tc.psum_pool(name="flip_psum", bufs=6))
@@ -77,8 +76,8 @@ def tile_minitransformerlayer_pa_kernel(tc, x, pe, w_qkv, g1, b1, out_0, out_1, 
         w_raw = {}
 
         def load_weights(n):
-            part, head_group = groups[n]
-            first = part * E + head_group * GROUP
+            part, pair = groups[n]
+            first = part * E + pair * GROUP
             raw = raw_pool.tile([P, ROWS * D], BF16, name="raw")
             nc.sync.dma_start(
                 out=raw[:], in_=w_qkv[first : first + GROUP, :].rearrange("(p r) k -> p (r k)", r=ROWS)
@@ -88,13 +87,11 @@ def tile_minitransformerlayer_pa_kernel(tc, x, pe, w_qkv, g1, b1, out_0, out_1, 
         for n in range(PREFETCH):
             load_weights(n)
 
-        pe_heads = pe_sb[:].unsqueeze(1).to_broadcast([P, GROUP_HEADS, P])
-        pe_pairs = (
-            pe_sb[:].rearrange("p (j i) -> p j i", i=2).unsqueeze(1).to_broadcast([P, GROUP_HEADS, P // 2, 2])
-        )
-        table_a = const.tile([P, GROUP_HEADS, P], F32)
-        nc.gpsimd.tensor_copy(out=table_a[:], in_=pe_heads)
-        table_b = const.tile([P, GROUP_HEADS, P // 2, 2], F32)
+        copies = BATCH * GROUP_HEADS
+        pe_pairs = pe_sb[:].rearrange("s (j i) -> s j i", i=2).unsqueeze(1).to_broadcast([P, copies, P // 2, 2])
+        table_a = const.tile([P, copies, P // 2, 2], F32)
+        nc.gpsimd.tensor_copy(out=table_a[:], in_=pe_pairs)
+        table_b = const.tile([P, copies, P // 2, 2], F32)
         nc.gpsimd.tensor_scalar(
             out=table_b[:, :, :, 0], in0=pe_pairs[:, :, :, 1], scalar1=-1.0, scalar2=0.0, op0=ALU.mult, op1=ALU.add
         )
@@ -102,11 +99,18 @@ def tile_minitransformerlayer_pa_kernel(tc, x, pe, w_qkv, g1, b1, out_0, out_1, 
 
         def repeat_on_partitions(row, name):
             repeated = const.tile([P, D], BF16, name=name)
-            for c in range(D // BANK):
-                cols = slice(c * BANK, (c + 1) * BANK)
-                spread = flip_psum.tile([P, BANK], F32, tag="flipped", name="spread")
-                nc.tensor.matmul(out=spread[:], lhsT=ones[:], rhs=row[:, cols], start=True, stop=True)
-                nc.scalar.copy(out=repeated[:, cols], in_=spread[:])
+            for bank in range(D // (2 * BANK)):
+                spread = flip_psum.tile([P, 2 * BANK], BF16, tag="flipped", name="spread")
+                for side in range(2):
+                    first = (2 * bank + side) * BANK
+                    nc.tensor.matmul(
+                        out=spread[:, side * BANK : (side + 1) * BANK],
+                        lhsT=ones[:],
+                        rhs=row[:, first : first + BANK],
+                        start=True,
+                        stop=True,
+                    )
+                nc.scalar.copy(out=repeated[:, 2 * bank * BANK : 2 * (bank + 1) * BANK], in_=spread[:])
             return repeated
 
         gain = repeat_on_partitions(gain_row, "gain")
@@ -120,7 +124,7 @@ def tile_minitransformerlayer_pa_kernel(tc, x, pe, w_qkv, g1, b1, out_0, out_1, 
             for c in range(D // BANK):
                 nc.vector.bn_stats(out=stats[:, c, :], in_=x_sb[b][:, c * BANK : (c + 1) * BANK])
             mv = norm.tile([P, 2], F32, name="mv")
-            nc.vector.bn_aggr(out=mv[:], in_=stats[:].rearrange("p c s -> p (c s)"))
+            nc.vector.bn_aggr(out=mv[:], in_=stats[:].rearrange("s c t -> s (c t)"))
             var_eps = norm.tile([P, 1], F32, name="var_eps")
             nc.vector.tensor_scalar_add(out=var_eps[:], in0=mv[:, 1:2], scalar1=EPS)
             root = norm.tile([P, 1], F32, name="root")
@@ -131,7 +135,7 @@ def tile_minitransformerlayer_pa_kernel(tc, x, pe, w_qkv, g1, b1, out_0, out_1, 
         h_sorted = {}
 
         def normalise(b):
-            centred = norm.tile([P, D], F32, name="centred")
+            centred = const.tile([P, D], F32, name="centred")
             nc.vector.scalar_tensor_tensor(
                 out=centred[:], in0=x_sb[b][:], scalar=mean_var[b][:, 0:1], in1=gain[:], op0=ALU.subtract, op1=ALU.mult
             )
@@ -141,9 +145,9 @@ def tile_minitransformerlayer_pa_kernel(tc, x, pe, w_qkv, g1, b1, out_0, out_1, 
             for e in range(2):
                 nc.vector.scalar_tensor_tensor(
                     out=h_tile[:, :, e, :],
-                    in0=centred[:].rearrange("p (cu q e) -> p cu e q", q=P, e=2)[:, :, e, :],
+                    in0=centred[:].rearrange("s (cu p e) -> s cu e p", p=P, e=2)[:, :, e, :],
                     scalar=rstd[:],
-                    in1=bias[:].rearrange("p (cu q e) -> p cu e q", q=P, e=2)[:, :, e, :],
+                    in1=bias[:].rearrange("s (cu p e) -> s cu e p", p=P, e=2)[:, :, e, :],
                     op0=ALU.mult,
                     op1=ALU.add,
                 )
@@ -159,120 +163,117 @@ def tile_minitransformerlayer_pa_kernel(tc, x, pe, w_qkv, g1, b1, out_0, out_1, 
                 for u in range(2):
                     for e in range(2):
                         nc.tensor.transpose(flipped_h[:, 2 * u + e, :], h_sorted[b][:, 2 * c + u, e, :], ident_bf16[:])
-                nc.scalar.copy(out=h_grouped[:, b, c, :, :], in_=flipped_h[:].rearrange("p t r -> p r t"))
+                nc.scalar.copy(out=h_grouped[:, b, c, :, :], in_=flipped_h[:].rearrange("p t s -> p s t"))
 
         def quantise_h(b):
             nc.vector.quantize_mx(
                 out=h_codes[:, b, :].bitcast(FP8X4),
                 scales=h_scales[:, b, :],
-                in_=h_grouped[:, b].rearrange("p c r t -> p (c r t)"),
+                in_=h_grouped[:, b].rearrange("p c s t -> p (c s t)"),
             )
 
         w_grouped = {}
 
-        def transpose_weights(n, half):
+        def transpose_weights(n):
             words = w_raw[n][:].bitcast(F32)
-            grouped = grouped_pool.tile([P, HALF, GROUP * PACK], BF16, align_bytes=64, name="grouped")
-            for c in range(HALF):
-                grouped_words = grouped[:, c, :].bitcast(F32)
-                for side in range(2):
-                    flipped = flip_psum.tile([P, 2, BANK // 2], F32, tag="flipped", name="flipped")
-                    for u in range(2):
-                        for r in range(2):
-                            first = (2 * side + r) * WORDS + (2 * (half * HALF + c) + u) * P
-                            nc.tensor.transpose(
-                                flipped[:, u, r * P : (r + 1) * P], words[:, first : first + P], ident_f32[:]
-                            )
-                    nc.scalar.copy(
-                        out=grouped_words[:, side * BANK : (side + 1) * BANK].rearrange("p (n u) -> p n u", u=2),
-                        in_=flipped[:].rearrange("p u n -> p n u"),
-                    )
-            w_grouped[(n, half)] = grouped
-            if half == 1 and n + PREFETCH < len(groups):
+            grouped = grouped_pool.tile([P, PASSES, GROUP * PACK], BF16, align_bytes=64, name="grouped")
+            for c in range(PASSES):
+                flipped = flip_psum.tile([P, 2, GROUP], F32, tag="flipped", name="flipped")
+                for u in range(2):
+                    for r in range(ROWS):
+                        first = r * WORDS + (2 * c + u) * P
+                        nc.tensor.transpose(flipped[:, u, r * P : (r + 1) * P], words[:, first : first + P], ident_f32[:])
+                nc.scalar.copy(
+                    out=grouped[:, c, :].bitcast(F32).rearrange("p (n u) -> p n u", u=2),
+                    in_=flipped[:].rearrange("p u n -> p n u"),
+                )
+            w_grouped[n] = grouped
+            if n + PREFETCH < len(groups):
                 load_weights(n + PREFETCH)
 
         w_codes = {}
         w_scales = {}
 
-        def quantise_weights(n, half):
-            codes = codes_pool.tile([P, HALF, GROUP], U32, align_bytes=64, name="codes")
-            scales = codes_pool.tile([P, HALF, GROUP], U8, align_bytes=64, name="scales")
+        def quantise_weights(n):
+            codes = codes_pool.tile([P, PASSES, GROUP], U32, align_bytes=64, name="codes")
+            scales = codes_pool.tile([P, PASSES, GROUP], U8, align_bytes=64, name="scales")
             nc.vector.quantize_mx(
                 out=codes[:].rearrange("p c n -> p (c n)").bitcast(FP8X4),
                 scales=scales[:].rearrange("p c n -> p (c n)"),
-                in_=w_grouped[(n, half)][:].rearrange("p c n -> p (c n)"),
+                in_=w_grouped[n][:].rearrange("p c n -> p (c n)"),
             )
-            w_codes[(n, half)] = codes
-            w_scales[(n, half)] = scales
+            w_codes[n] = codes
+            w_scales[n] = scales
 
         products = {}
 
-        def multiply(n, b):
-            acc = acc_psum.tile([P, BANK], F32, name="acc")
-            for c in range(PASSES):
-                tokens = slice(c * P, (c + 1) * P)
-                nc.tensor.matmul_mx(
-                    out=acc[:],
-                    lhsT=h_codes[:, b, tokens].bitcast(FP8X4),
-                    lhsT_scale=h_scales[:, b, tokens],
-                    rhs=w_codes[(n, c // HALF)][:, c % HALF, :].bitcast(FP8X4),
-                    rhs_scale=w_scales[(n, c // HALF)][:, c % HALF, :],
-                    start=(c == 0),
-                    stop=(c == PASSES - 1),
-                )
-            products[(n, b)] = acc
+        def multiply(n):
+            acc = acc_psum.tile([P, BATCH, GROUP], F32, name="acc")
+            for b in range(BATCH):
+                for c in range(PASSES):
+                    tokens = slice(c * P, (c + 1) * P)
+                    nc.tensor.matmul_mx(
+                        out=acc[:, b, :],
+                        lhsT=h_codes[:, b, tokens].bitcast(FP8X4),
+                        lhsT_scale=h_scales[:, b, tokens],
+                        rhs=w_codes[n][:, c, :].bitcast(FP8X4),
+                        rhs_scale=w_scales[n][:, c, :],
+                        start=(c == 0),
+                        stop=(c == PASSES - 1),
+                    )
+            products[n] = acc
 
-        def finish(n, b):
-            part, head_group = groups[n]
-            heads = slice(head_group * GROUP_HEADS, (head_group + 1) * GROUP_HEADS)
-            acc = products[(n, b)]
-            result = result_pool.tile([P, GROUP], F32, name="result")
+        def finish(n):
+            part, pair = groups[n]
+            heads = slice(pair * GROUP_HEADS, (pair + 1) * GROUP_HEADS)
+            acc = products[n]
+            result = result_pool.tile([P, BATCH, GROUP], F32, name="result")
             if part == 2:
                 nc.vector.tensor_copy(
-                    out=result[:].rearrange("s (p r) -> s p r", r=ROWS),
-                    in_=acc[:].rearrange("s (r p) -> s p r", r=ROWS),
+                    out=result[:].rearrange("s b (p r) -> s b p r", r=ROWS),
+                    in_=acc[:].rearrange("s b (r p) -> s b p r", r=ROWS),
                 )
             else:
-                pairs = acc[:].rearrange("s (v i p) -> s i p v", v=2, i=2)
-                shape = [P, P, 2, 2]
-                from_a = rot_pool.tile([P, GROUP], F32, name="from_a")
+                halves = acc[:].rearrange("s b (r p) -> s r b p", r=ROWS)
+                shape = [P, BATCH, P, 2]
+                from_a = rot_pool.tile([P, BATCH, P, 2], F32, name="from_a")
                 nc.vector.tensor_mul(
-                    out=from_a[:].rearrange("s (p v i) -> s p v i", v=2, i=2),
-                    in0=pairs[:, 0].unsqueeze(3).to_broadcast(shape),
-                    in1=table_a[:].rearrange("s h (q v i) -> s (h q) v i", v=2, i=2),
+                    out=from_a[:],
+                    in0=halves[:, 0].unsqueeze(3).to_broadcast(shape),
+                    in1=table_a[:].rearrange("s (b h) j i -> s b (h j) i", b=BATCH),
                 )
-                from_b = rot_pool.tile([P, GROUP], F32, name="from_b")
+                from_b = rot_pool.tile([P, BATCH, P, 2], F32, name="from_b")
                 nc.vector.tensor_mul(
-                    out=from_b[:].rearrange("s (p v i) -> s p v i", v=2, i=2),
-                    in0=pairs[:, 1].unsqueeze(3).to_broadcast(shape),
-                    in1=table_b[:].rearrange("s h (q v) i -> s (h q) v i", v=2),
+                    out=from_b[:],
+                    in0=halves[:, 1].unsqueeze(3).to_broadcast(shape),
+                    in1=table_b[:].rearrange("s (b h) j i -> s b (h j) i", b=BATCH),
                 )
-                nc.gpsimd.tensor_add(out=result[:], in0=from_a[:], in1=from_b[:])
-            nc.sync.dma_start(
-                out=outs[part][b, heads].rearrange("h s d -> s h d"),
-                in_=result[:].rearrange("s (h d) -> s h d", d=P),
-            )
+                nc.gpsimd.tensor_add(
+                    out=result[:].rearrange("s b (p i) -> s b p i", i=2), in0=from_a[:], in1=from_b[:]
+                )
+            for b in range(BATCH):
+                nc.sync.dma_start(
+                    out=outs[part][b, heads].rearrange("h s d -> s h d"),
+                    in_=result[:, b, :].rearrange("s (h d) -> s h d", d=P),
+                )
 
-        halves = [(n, half) for n in range(len(groups)) for half in range(2)]
-        token_statistics(0)
-        token_statistics(1)
-        transpose_weights(0, 0)
-        transpose_weights(0, 1)
-        normalise(0)
-        transpose_h(0)
-        transpose_weights(1, 0)
-        transpose_weights(1, 1)
-        normalise(1)
-        transpose_h(1)
-        quantise_weights(0, 0)
-        quantise_weights(0, 1)
-        quantise_h(0)
-        quantise_h(1)
-        for t in range(len(halves)):
-            n, b = halves[t]
-            multiply(n, b)
-            if t + 2 * AHEAD - LAG < len(halves):
-                quantise_weights(*halves[t + 2 * AHEAD - LAG])
-            finish(n, b)
-            if t + 2 * AHEAD < len(halves):
-                transpose_weights(*halves[t + 2 * AHEAD])
+        transpose_weights(0)
+        for b in range(BATCH):
+            token_statistics(b)
+        for n in range(1, AHEAD):
+            transpose_weights(n)
+        for b in range(BATCH):
+            normalise(b)
+            transpose_h(b)
+        quantise_weights(0)
+        for b in range(BATCH):
+            quantise_h(b)
+        for n in range(1, AHEAD - LAG):
+            quantise_weights(n)
+        for n in range(len(groups)):
+            multiply(n)
+            if n + AHEAD - LAG < len(groups):
+                quantise_weights(n + AHEAD - LAG)
+            finish(n)
+            if n + AHEAD < len(groups):
+                transpose_weights(n + AHEAD)

@@ -20,12 +20,13 @@ EPS = 1e-5
 PACK = 4
 PASSES = D // (P * PACK)
 BANK = 512
-WORDS = D // 2
-GROUP = BANK // BATCH
+GROUP = BANK
 ROWS = GROUP // P
 GROUP_HEADS = GROUP // P
-PREFETCH = 10
-AHEAD = 4
+WORDS = D // 2
+PREFETCH = 4
+AHEAD = 2
+HALF = PASSES // 2
 LAG = 2
 
 FLOPS = 2 * BATCH * P * D * 3 * E
@@ -34,14 +35,14 @@ FLOPS = 2 * BATCH * P * D * 3 * E
 def tile_minitransformerlayer_pa_kernel(tc, x, pe, w_qkv, g1, b1, out_0, out_1, out_2):
     nc = tc.nc
     outs = (out_0, out_1, out_2)
-    groups = [(part, pair) for pair in range(HEADS // GROUP_HEADS) for part in range(3)]
+    groups = [(part, head_group) for head_group in range(HEADS // GROUP_HEADS) for part in range(3)]
 
     with ExitStack() as ctx:
         const = ctx.enter_context(tc.tile_pool(name="const", bufs=1))
         norm = ctx.enter_context(tc.tile_pool(name="norm", bufs=BATCH))
         raw_pool = ctx.enter_context(tc.tile_pool(name="raw", bufs=PREFETCH))
-        grouped_pool = ctx.enter_context(tc.tile_pool(name="grouped", bufs=AHEAD))
-        codes_pool = ctx.enter_context(tc.tile_pool(name="codes", bufs=AHEAD))
+        grouped_pool = ctx.enter_context(tc.tile_pool(name="grouped", bufs=4))
+        codes_pool = ctx.enter_context(tc.tile_pool(name="codes", bufs=6))
         rot_pool = ctx.enter_context(tc.tile_pool(name="rot", bufs=3))
         result_pool = ctx.enter_context(tc.tile_pool(name="result", bufs=8))
         flip_psum = ctx.enter_context(tc.psum_pool(name="flip_psum", bufs=6))
@@ -67,7 +68,9 @@ def tile_minitransformerlayer_pa_kernel(tc, x, pe, w_qkv, g1, b1, out_0, out_1, 
         x_sb = {}
         for b in range(BATCH):
             x_tile = norm.tile([P, D], BF16, name="x_tile")
-            nc.sync.dma_start(out=x_tile[:], in_=x[b])
+            for c in range(D // BANK):
+                cols = slice(c * BANK, (c + 1) * BANK)
+                nc.sync.dma_start(out=x_tile[:, cols], in_=x[b][:, cols])
             x_sb[b] = x_tile
         nc.sync.dma_start(out=gain_row[0:1, :], in_=g1.rearrange("(o d) -> o d", o=1))
         nc.sync.dma_start(out=bias_row[0:1, :], in_=b1.rearrange("(o d) -> o d", o=1))
@@ -76,8 +79,8 @@ def tile_minitransformerlayer_pa_kernel(tc, x, pe, w_qkv, g1, b1, out_0, out_1, 
         w_raw = {}
 
         def load_weights(n):
-            part, pair = groups[n]
-            first = part * E + pair * GROUP
+            part, head_group = groups[n]
+            first = part * E + head_group * GROUP
             raw = raw_pool.tile([P, ROWS * D], BF16, name="raw")
             nc.sync.dma_start(
                 out=raw[:], in_=w_qkv[first : first + GROUP, :].rearrange("(p r) k -> p (r k)", r=ROWS)
@@ -87,11 +90,13 @@ def tile_minitransformerlayer_pa_kernel(tc, x, pe, w_qkv, g1, b1, out_0, out_1, 
         for n in range(PREFETCH):
             load_weights(n)
 
-        copies = BATCH * GROUP_HEADS
-        pe_pairs = pe_sb[:].rearrange("s (j i) -> s j i", i=2).unsqueeze(1).to_broadcast([P, copies, P // 2, 2])
-        table_a = const.tile([P, copies, P // 2, 2], F32)
-        nc.gpsimd.tensor_copy(out=table_a[:], in_=pe_pairs)
-        table_b = const.tile([P, copies, P // 2, 2], F32)
+        pe_heads = pe_sb[:].unsqueeze(1).to_broadcast([P, GROUP_HEADS, P])
+        pe_pairs = (
+            pe_sb[:].rearrange("p (j i) -> p j i", i=2).unsqueeze(1).to_broadcast([P, GROUP_HEADS, P // 2, 2])
+        )
+        table_a = const.tile([P, GROUP_HEADS, P], F32)
+        nc.gpsimd.tensor_copy(out=table_a[:], in_=pe_heads)
+        table_b = const.tile([P, GROUP_HEADS, P // 2, 2], F32)
         nc.gpsimd.tensor_scalar(
             out=table_b[:, :, :, 0], in0=pe_pairs[:, :, :, 1], scalar1=-1.0, scalar2=0.0, op0=ALU.mult, op1=ALU.add
         )
@@ -124,7 +129,7 @@ def tile_minitransformerlayer_pa_kernel(tc, x, pe, w_qkv, g1, b1, out_0, out_1, 
             for c in range(D // BANK):
                 nc.vector.bn_stats(out=stats[:, c, :], in_=x_sb[b][:, c * BANK : (c + 1) * BANK])
             mv = norm.tile([P, 2], F32, name="mv")
-            nc.vector.bn_aggr(out=mv[:], in_=stats[:].rearrange("s c t -> s (c t)"))
+            nc.vector.bn_aggr(out=mv[:], in_=stats[:].rearrange("p c s -> p (c s)"))
             var_eps = norm.tile([P, 1], F32, name="var_eps")
             nc.vector.tensor_scalar_add(out=var_eps[:], in0=mv[:, 1:2], scalar1=EPS)
             root = norm.tile([P, 1], F32, name="root")
@@ -145,9 +150,9 @@ def tile_minitransformerlayer_pa_kernel(tc, x, pe, w_qkv, g1, b1, out_0, out_1, 
             for e in range(2):
                 nc.vector.scalar_tensor_tensor(
                     out=h_tile[:, :, e, :],
-                    in0=centred[:].rearrange("s (cu p e) -> s cu e p", p=P, e=2)[:, :, e, :],
+                    in0=centred[:].rearrange("p (cu q e) -> p cu e q", q=P, e=2)[:, :, e, :],
                     scalar=rstd[:],
-                    in1=bias[:].rearrange("s (cu p e) -> s cu e p", p=P, e=2)[:, :, e, :],
+                    in1=bias[:].rearrange("p (cu q e) -> p cu e q", q=P, e=2)[:, :, e, :],
                     op0=ALU.mult,
                     op1=ALU.add,
                 )
@@ -163,117 +168,120 @@ def tile_minitransformerlayer_pa_kernel(tc, x, pe, w_qkv, g1, b1, out_0, out_1, 
                 for u in range(2):
                     for e in range(2):
                         nc.tensor.transpose(flipped_h[:, 2 * u + e, :], h_sorted[b][:, 2 * c + u, e, :], ident_bf16[:])
-                nc.scalar.copy(out=h_grouped[:, b, c, :, :], in_=flipped_h[:].rearrange("p t s -> p s t"))
+                nc.scalar.copy(out=h_grouped[:, b, c, :, :], in_=flipped_h[:].rearrange("p t r -> p r t"))
 
         def quantise_h(b):
             nc.vector.quantize_mx(
                 out=h_codes[:, b, :].bitcast(FP8X4),
                 scales=h_scales[:, b, :],
-                in_=h_grouped[:, b].rearrange("p c s t -> p (c s t)"),
+                in_=h_grouped[:, b].rearrange("p c r t -> p (c r t)"),
             )
 
         w_grouped = {}
 
-        def transpose_weights(n):
+        def transpose_weights(n, half):
             words = w_raw[n][:].bitcast(F32)
-            grouped = grouped_pool.tile([P, PASSES, GROUP * PACK], BF16, align_bytes=64, name="grouped")
-            for c in range(PASSES):
-                flipped = flip_psum.tile([P, 2, GROUP], F32, tag="flipped", name="flipped")
-                for u in range(2):
-                    for r in range(ROWS):
-                        first = r * WORDS + (2 * c + u) * P
-                        nc.tensor.transpose(flipped[:, u, r * P : (r + 1) * P], words[:, first : first + P], ident_f32[:])
-                nc.scalar.copy(
-                    out=grouped[:, c, :].bitcast(F32).rearrange("p (n u) -> p n u", u=2),
-                    in_=flipped[:].rearrange("p u n -> p n u"),
-                )
-            w_grouped[n] = grouped
-            if n + PREFETCH < len(groups):
+            grouped = grouped_pool.tile([P, HALF, GROUP * PACK], BF16, align_bytes=64, name="grouped")
+            for c in range(HALF):
+                grouped_words = grouped[:, c, :].bitcast(F32)
+                for side in range(2):
+                    flipped = flip_psum.tile([P, 2, BANK // 2], F32, tag="flipped", name="flipped")
+                    for u in range(2):
+                        for r in range(2):
+                            first = (2 * side + r) * WORDS + (2 * (half * HALF + c) + u) * P
+                            nc.tensor.transpose(
+                                flipped[:, u, r * P : (r + 1) * P], words[:, first : first + P], ident_f32[:]
+                            )
+                    nc.scalar.copy(
+                        out=grouped_words[:, side * BANK : (side + 1) * BANK].rearrange("p (n u) -> p n u", u=2),
+                        in_=flipped[:].rearrange("p u n -> p n u"),
+                    )
+            w_grouped[(n, half)] = grouped
+            if half == 1 and n + PREFETCH < len(groups):
                 load_weights(n + PREFETCH)
 
         w_codes = {}
         w_scales = {}
 
-        def quantise_weights(n):
-            codes = codes_pool.tile([P, PASSES, GROUP], U32, align_bytes=64, name="codes")
-            scales = codes_pool.tile([P, PASSES, GROUP], U8, align_bytes=64, name="scales")
+        def quantise_weights(n, half):
+            codes = codes_pool.tile([P, HALF, GROUP], U32, align_bytes=64, name="codes")
+            scales = codes_pool.tile([P, HALF, GROUP], U8, align_bytes=64, name="scales")
             nc.vector.quantize_mx(
                 out=codes[:].rearrange("p c n -> p (c n)").bitcast(FP8X4),
                 scales=scales[:].rearrange("p c n -> p (c n)"),
-                in_=w_grouped[n][:].rearrange("p c n -> p (c n)"),
+                in_=w_grouped[(n, half)][:].rearrange("p c n -> p (c n)"),
             )
-            w_codes[n] = codes
-            w_scales[n] = scales
+            w_codes[(n, half)] = codes
+            w_scales[(n, half)] = scales
 
         products = {}
 
-        def multiply(n):
-            acc = acc_psum.tile([P, BATCH, GROUP], F32, name="acc")
-            for b in range(BATCH):
-                for c in range(PASSES):
-                    tokens = slice(c * P, (c + 1) * P)
-                    nc.tensor.matmul_mx(
-                        out=acc[:, b, :],
-                        lhsT=h_codes[:, b, tokens].bitcast(FP8X4),
-                        lhsT_scale=h_scales[:, b, tokens],
-                        rhs=w_codes[n][:, c, :].bitcast(FP8X4),
-                        rhs_scale=w_scales[n][:, c, :],
-                        start=(c == 0),
-                        stop=(c == PASSES - 1),
-                    )
-            products[n] = acc
+        def multiply(n, b):
+            acc = acc_psum.tile([P, BANK], F32, name="acc")
+            for c in range(PASSES):
+                tokens = slice(c * P, (c + 1) * P)
+                nc.tensor.matmul_mx(
+                    out=acc[:],
+                    lhsT=h_codes[:, b, tokens].bitcast(FP8X4),
+                    lhsT_scale=h_scales[:, b, tokens],
+                    rhs=w_codes[(n, c // HALF)][:, c % HALF, :].bitcast(FP8X4),
+                    rhs_scale=w_scales[(n, c // HALF)][:, c % HALF, :],
+                    start=(c == 0),
+                    stop=(c == PASSES - 1),
+                )
+            products[(n, b)] = acc
 
-        def finish(n):
-            part, pair = groups[n]
-            heads = slice(pair * GROUP_HEADS, (pair + 1) * GROUP_HEADS)
-            acc = products[n]
-            result = result_pool.tile([P, BATCH, GROUP], F32, name="result")
+        def finish(n, b):
+            part, head_group = groups[n]
+            heads = slice(head_group * GROUP_HEADS, (head_group + 1) * GROUP_HEADS)
+            acc = products[(n, b)]
+            result = result_pool.tile([P, GROUP], F32, name="result")
             if part == 2:
                 nc.vector.tensor_copy(
-                    out=result[:].rearrange("s b (p r) -> s b p r", r=ROWS),
-                    in_=acc[:].rearrange("s b (r p) -> s b p r", r=ROWS),
+                    out=result[:].rearrange("s (p r) -> s p r", r=ROWS),
+                    in_=acc[:].rearrange("s (r p) -> s p r", r=ROWS),
                 )
             else:
-                halves = acc[:].rearrange("s b (r p) -> s r b p", r=ROWS)
-                shape = [P, BATCH, P, 2]
-                from_a = rot_pool.tile([P, BATCH, P, 2], F32, name="from_a")
+                pairs = acc[:].rearrange("s (v i p) -> s i p v", v=2, i=2)
+                shape = [P, P, 2, 2]
+                from_a = rot_pool.tile([P, GROUP], F32, name="from_a")
                 nc.vector.tensor_mul(
-                    out=from_a[:],
-                    in0=halves[:, 0].unsqueeze(3).to_broadcast(shape),
-                    in1=table_a[:].rearrange("s (b h) j i -> s b (h j) i", b=BATCH),
+                    out=from_a[:].rearrange("s (p v i) -> s p v i", v=2, i=2),
+                    in0=pairs[:, 0].unsqueeze(3).to_broadcast(shape),
+                    in1=table_a[:].rearrange("s h (q v i) -> s (h q) v i", v=2, i=2),
                 )
-                from_b = rot_pool.tile([P, BATCH, P, 2], F32, name="from_b")
+                from_b = rot_pool.tile([P, GROUP], F32, name="from_b")
                 nc.vector.tensor_mul(
-                    out=from_b[:],
-                    in0=halves[:, 1].unsqueeze(3).to_broadcast(shape),
-                    in1=table_b[:].rearrange("s (b h) j i -> s b (h j) i", b=BATCH),
+                    out=from_b[:].rearrange("s (p v i) -> s p v i", v=2, i=2),
+                    in0=pairs[:, 1].unsqueeze(3).to_broadcast(shape),
+                    in1=table_b[:].rearrange("s h (q v) i -> s (h q) v i", v=2),
                 )
-                nc.gpsimd.tensor_add(
-                    out=result[:].rearrange("s b (p i) -> s b p i", i=2), in0=from_a[:], in1=from_b[:]
-                )
-            for b in range(BATCH):
-                nc.sync.dma_start(
-                    out=outs[part][b, heads].rearrange("h s d -> s h d"),
-                    in_=result[:, b, :].rearrange("s (h d) -> s h d", d=P),
-                )
+                nc.gpsimd.tensor_add(out=result[:], in0=from_a[:], in1=from_b[:])
+            nc.sync.dma_start(
+                out=outs[part][b, heads].rearrange("h s d -> s h d"),
+                in_=result[:].rearrange("s (h d) -> s h d", d=P),
+            )
 
-        transpose_weights(0)
-        for b in range(BATCH):
-            token_statistics(b)
-        for n in range(1, AHEAD):
-            transpose_weights(n)
-        for b in range(BATCH):
-            normalise(b)
-            transpose_h(b)
-        quantise_weights(0)
-        for b in range(BATCH):
-            quantise_h(b)
-        for n in range(1, AHEAD - LAG):
-            quantise_weights(n)
-        for n in range(len(groups)):
-            multiply(n)
-            if n + AHEAD - LAG < len(groups):
-                quantise_weights(n + AHEAD - LAG)
-            finish(n)
-            if n + AHEAD < len(groups):
-                transpose_weights(n + AHEAD)
+        halves = [(n, half) for n in range(len(groups)) for half in range(2)]
+        token_statistics(0)
+        token_statistics(1)
+        transpose_weights(0, 0)
+        transpose_weights(0, 1)
+        normalise(0)
+        transpose_h(0)
+        transpose_weights(1, 0)
+        transpose_weights(1, 1)
+        normalise(1)
+        transpose_h(1)
+        quantise_weights(0, 0)
+        quantise_weights(0, 1)
+        quantise_h(0)
+        quantise_h(1)
+        for t in range(len(halves)):
+            n, b = halves[t]
+            multiply(n, b)
+            if t + 2 * AHEAD - LAG < len(halves):
+                quantise_weights(*halves[t + 2 * AHEAD - LAG])
+            finish(n, b)
+            if t + 2 * AHEAD < len(halves):
+                transpose_weights(*halves[t + 2 * AHEAD])

from contextlib import ExitStack

import concourse.mybir as mybir
from concourse.masks import make_identity

F32 = mybir.dt.float32
BF16 = mybir.dt.bfloat16
I32 = mybir.dt.int32
U32 = mybir.dt.uint32
U8 = mybir.dt.uint8
FP8X4 = mybir.dt.float8_e4m3fn_x4
ALU = mybir.AluOpType

P = 128
BATCH = 2
D = 2048
HEADS = 16
E = HEADS * P
EPS = 1e-5
PACK = 4
PASSES = D // (P * PACK)
BANK = 512
GROUP = BANK
ROWS = GROUP // P
GROUP_HEADS = GROUP // P
WORDS = D // 2
PREFETCH = 4
AHEAD = 2
HALF = PASSES // 2
LAG = 2

FLOPS = 2 * BATCH * P * D * 3 * E


def tile_minitransformerlayer_pa_kernel(tc, x, pe, w_qkv, g1, b1, out_0, out_1, out_2):
    nc = tc.nc
    outs = (out_0, out_1, out_2)
    groups = [(part, head_group) for head_group in range(HEADS // GROUP_HEADS) for part in range(3)]

    with ExitStack() as ctx:
        const = ctx.enter_context(tc.tile_pool(name="const", bufs=1))
        norm = ctx.enter_context(tc.tile_pool(name="norm", bufs=BATCH))
        raw_pool = ctx.enter_context(tc.tile_pool(name="raw", bufs=PREFETCH))
        grouped_pool = ctx.enter_context(tc.tile_pool(name="grouped", bufs=4))
        codes_pool = ctx.enter_context(tc.tile_pool(name="codes", bufs=6))
        rot_pool = ctx.enter_context(tc.tile_pool(name="rot", bufs=3))
        result_pool = ctx.enter_context(tc.tile_pool(name="result", bufs=8))
        flip_psum = ctx.enter_context(tc.psum_pool(name="flip_psum", bufs=6))
        acc_psum = ctx.enter_context(tc.psum_pool(name="acc_psum", bufs=2))
        ctx.enter_context(tc.manual_schedule())

        one = const.tile([P, 1], F32)
        nc.vector.memset(one[:], 1.0)
        warm = const.tile([P, 1], F32)
        nc.scalar.sqrt(out=warm[:], in_=one[:])
        ones = const.tile([P, P], BF16)
        nc.vector.memset(ones[:], 1.0)
        gain_row = const.tile([P, D], BF16)
        bias_row = const.tile([P, D], BF16)
        nc.vector.memset(gain_row[:].bitcast(I32), 0)
        nc.vector.memset(bias_row[:].bitcast(I32), 0)
        pe_sb = const.tile([P, P], BF16)
        ident_f32 = const.tile([P, P], F32)
        make_identity(nc, ident_f32[:])
        ident_bf16 = const.tile([P, P], BF16)
        make_identity(nc, ident_bf16[:])

        x_sb = {}
        for b in range(BATCH):
            x_tile = norm.tile([P, D], BF16, name="x_tile")
            for c in range(D // BANK):
                cols = slice(c * BANK, (c + 1) * BANK)
                nc.sync.dma_start(out=x_tile[:, cols], in_=x[b][:, cols])
            x_sb[b] = x_tile
        nc.sync.dma_start(out=gain_row[0:1, :], in_=g1.rearrange("(o d) -> o d", o=1))
        nc.sync.dma_start(out=bias_row[0:1, :], in_=b1.rearrange("(o d) -> o d", o=1))
        nc.sync.dma_start(out=pe_sb[:], in_=pe)

        w_raw = {}

        def load_weights(n):
            part, head_group = groups[n]
            first = part * E + head_group * GROUP
            raw = raw_pool.tile([P, ROWS * D], BF16, name="raw")
            nc.sync.dma_start(
                out=raw[:], in_=w_qkv[first : first + GROUP, :].rearrange("(p r) k -> p (r k)", r=ROWS)
            )
            w_raw[n] = raw

        for n in range(PREFETCH):
            load_weights(n)

        pe_heads = pe_sb[:].unsqueeze(1).to_broadcast([P, GROUP_HEADS, P])
        pe_pairs = (
            pe_sb[:].rearrange("p (j i) -> p j i", i=2).unsqueeze(1).to_broadcast([P, GROUP_HEADS, P // 2, 2])
        )
        table_a = const.tile([P, GROUP_HEADS, P], F32)
        nc.gpsimd.tensor_copy(out=table_a[:], in_=pe_heads)
        table_b = const.tile([P, GROUP_HEADS, P // 2, 2], F32)
        nc.gpsimd.tensor_scalar(
            out=table_b[:, :, :, 0], in0=pe_pairs[:, :, :, 1], scalar1=-1.0, scalar2=0.0, op0=ALU.mult, op1=ALU.add
        )
        nc.gpsimd.tensor_copy(out=table_b[:, :, :, 1], in_=pe_pairs[:, :, :, 0])

        def repeat_on_partitions(row, name):
            repeated = const.tile([P, D], BF16, name=name)
            for bank in range(D // (2 * BANK)):
                spread = flip_psum.tile([P, 2 * BANK], BF16, tag="flipped", name="spread")
                for side in range(2):
                    first = (2 * bank + side) * BANK
                    nc.tensor.matmul(
                        out=spread[:, side * BANK : (side + 1) * BANK],
                        lhsT=ones[:],
                        rhs=row[:, first : first + BANK],
                        start=True,
                        stop=True,
                    )
                nc.scalar.copy(out=repeated[:, 2 * bank * BANK : 2 * (bank + 1) * BANK], in_=spread[:])
            return repeated

        gain = repeat_on_partitions(gain_row, "gain")
        bias = repeat_on_partitions(bias_row, "bias")

        mean_var = {}
        std = {}

        def token_statistics(b):
            stats = norm.tile([P, D // BANK, 6], F32, name="stats")
            for c in range(D // BANK):
                nc.vector.bn_stats(out=stats[:, c, :], in_=x_sb[b][:, c * BANK : (c + 1) * BANK])
            mv = norm.tile([P, 2], F32, name="mv")
            nc.vector.bn_aggr(out=mv[:], in_=stats[:].rearrange("p c s -> p (c s)"))
            var_eps = norm.tile([P, 1], F32, name="var_eps")
            nc.vector.tensor_scalar_add(out=var_eps[:], in0=mv[:, 1:2], scalar1=EPS)
            root = norm.tile([P, 1], F32, name="root")
            nc.scalar.sqrt(out=root[:], in_=var_eps[:])
            mean_var[b] = mv
            std[b] = root

        h_sorted = {}

        def normalise(b):
            centred = const.tile([P, D], F32, name="centred")
            nc.vector.scalar_tensor_tensor(
                out=centred[:], in0=x_sb[b][:], scalar=mean_var[b][:, 0:1], in1=gain[:], op0=ALU.subtract, op1=ALU.mult
            )
            rstd = norm.tile([P, 1], F32, name="rstd")
            nc.vector.reciprocal(out=rstd[:], in_=std[b][:])
            h_tile = norm.tile([P, 2 * PASSES, 2, P], BF16, name="h_tile")
            for e in range(2):
                nc.vector.scalar_tensor_tensor(
                    out=h_tile[:, :, e, :],
                    in0=centred[:].rearrange("p (cu q e) -> p cu e q", q=P, e=2)[:, :, e, :],
                    scalar=rstd[:],
                    in1=bias[:].rearrange("p (cu q e) -> p cu e q", q=P, e=2)[:, :, e, :],
                    op0=ALU.mult,
                    op1=ALU.add,
                )
            h_sorted[b] = h_tile

        h_grouped = const.tile([P, BATCH, PASSES, P, PACK], BF16, align_bytes=64)
        h_codes = const.tile([P, BATCH, PASSES * P], U32, align_bytes=64)
        h_scales = const.tile([P, BATCH, PASSES * P], U8, align_bytes=64)

        def transpose_h(b):
            for c in range(PASSES):
                flipped_h = flip_psum.tile([P, PACK, P], BF16, tag="flipped", name="flipped_h")
                for u in range(2):
                    for e in range(2):
                        nc.tensor.transpose(flipped_h[:, 2 * u + e, :], h_sorted[b][:, 2 * c + u, e, :], ident_bf16[:])
                nc.scalar.copy(out=h_grouped[:, b, c, :, :], in_=flipped_h[:].rearrange("p t r -> p r t"))

        def quantise_h(b):
            nc.vector.quantize_mx(
                out=h_codes[:, b, :].bitcast(FP8X4),
                scales=h_scales[:, b, :],
                in_=h_grouped[:, b].rearrange("p c r t -> p (c r t)"),
            )

        w_grouped = {}

        def transpose_weights(n, half):
            words = w_raw[n][:].bitcast(F32)
            grouped = grouped_pool.tile([P, HALF, GROUP * PACK], BF16, align_bytes=64, name="grouped")
            for c in range(HALF):
                grouped_words = grouped[:, c, :].bitcast(F32)
                for side in range(2):
                    flipped = flip_psum.tile([P, 2, BANK // 2], F32, tag="flipped", name="flipped")
                    for u in range(2):
                        for r in range(2):
                            first = (2 * side + r) * WORDS + (2 * (half * HALF + c) + u) * P
                            nc.tensor.transpose(
                                flipped[:, u, r * P : (r + 1) * P], words[:, first : first + P], ident_f32[:]
                            )
                    nc.scalar.copy(
                        out=grouped_words[:, side * BANK : (side + 1) * BANK].rearrange("p (n u) -> p n u", u=2),
                        in_=flipped[:].rearrange("p u n -> p n u"),
                    )
            w_grouped[(n, half)] = grouped
            if half == 1 and n + PREFETCH < len(groups):
                load_weights(n + PREFETCH)

        w_codes = {}
        w_scales = {}

        def quantise_weights(n, half):
            codes = codes_pool.tile([P, HALF, GROUP], U32, align_bytes=64, name="codes")
            scales = codes_pool.tile([P, HALF, GROUP], U8, align_bytes=64, name="scales")
            nc.vector.quantize_mx(
                out=codes[:].rearrange("p c n -> p (c n)").bitcast(FP8X4),
                scales=scales[:].rearrange("p c n -> p (c n)"),
                in_=w_grouped[(n, half)][:].rearrange("p c n -> p (c n)"),
            )
            w_codes[(n, half)] = codes
            w_scales[(n, half)] = scales

        products = {}

        def multiply(n, b):
            acc = acc_psum.tile([P, BANK], F32, name="acc")
            for c in range(PASSES):
                tokens = slice(c * P, (c + 1) * P)
                nc.tensor.matmul_mx(
                    out=acc[:],
                    lhsT=h_codes[:, b, tokens].bitcast(FP8X4),
                    lhsT_scale=h_scales[:, b, tokens],
                    rhs=w_codes[(n, c // HALF)][:, c % HALF, :].bitcast(FP8X4),
                    rhs_scale=w_scales[(n, c // HALF)][:, c % HALF, :],
                    start=(c == 0),
                    stop=(c == PASSES - 1),
                )
            products[(n, b)] = acc

        def finish(n, b):
            part, head_group = groups[n]
            heads = slice(head_group * GROUP_HEADS, (head_group + 1) * GROUP_HEADS)
            acc = products[(n, b)]
            result = result_pool.tile([P, GROUP], F32, name="result")
            if part == 2:
                nc.vector.tensor_copy(
                    out=result[:].rearrange("s (p r) -> s p r", r=ROWS),
                    in_=acc[:].rearrange("s (r p) -> s p r", r=ROWS),
                )
            else:
                pairs = acc[:].rearrange("s (v i p) -> s i p v", v=2, i=2)
                shape = [P, P, 2, 2]
                from_a = rot_pool.tile([P, GROUP], F32, name="from_a")
                nc.vector.tensor_mul(
                    out=from_a[:].rearrange("s (p v i) -> s p v i", v=2, i=2),
                    in0=pairs[:, 0].unsqueeze(3).to_broadcast(shape),
                    in1=table_a[:].rearrange("s h (q v i) -> s (h q) v i", v=2, i=2),
                )
                from_b = rot_pool.tile([P, GROUP], F32, name="from_b")
                nc.vector.tensor_mul(
                    out=from_b[:].rearrange("s (p v i) -> s p v i", v=2, i=2),
                    in0=pairs[:, 1].unsqueeze(3).to_broadcast(shape),
                    in1=table_b[:].rearrange("s h (q v) i -> s (h q) v i", v=2),
                )
                nc.gpsimd.tensor_add(out=result[:], in0=from_a[:], in1=from_b[:])
            nc.sync.dma_start(
                out=outs[part][b, heads].rearrange("h s d -> s h d"),
                in_=result[:].rearrange("s (h d) -> s h d", d=P),
            )

        halves = [(n, half) for n in range(len(groups)) for half in range(2)]
        token_statistics(0)
        token_statistics(1)
        transpose_weights(0, 0)
        transpose_weights(0, 1)
        normalise(0)
        transpose_h(0)
        transpose_weights(1, 0)
        transpose_weights(1, 1)
        normalise(1)
        transpose_h(1)
        quantise_weights(0, 0)
        quantise_weights(0, 1)
        quantise_h(0)
        quantise_h(1)
        for t in range(len(halves)):
            n, b = halves[t]
            multiply(n, b)
            if t + 2 * AHEAD - LAG < len(halves):
                quantise_weights(*halves[t + 2 * AHEAD - LAG])
            finish(n, b)
            if t + 2 * AHEAD < len(halves):
                transpose_weights(*halves[t + 2 * AHEAD])
